import numpy as np
import ml_dtypes


def mxq(x, axis, fmt="e4m3"):
    dtype, down = {"e4m3": (ml_dtypes.float8_e4m3fn, 7), "e5m2": (ml_dtypes.float8_e5m2, 14)}[fmt]
    v = np.moveaxis(np.asarray(x, np.float32).astype(ml_dtypes.bfloat16).astype(np.float64), axis, -1)
    blocks = v.reshape(v.shape[:-1] + (-1, 32))
    amax = np.abs(blocks).max(-1, keepdims=True)
    byte = np.maximum(np.where(amax > 0, np.frexp(amax)[1] - 1 + 127, 0) - down, 1)
    scale = np.exp2(byte - 127.0)
    codes = (blocks / scale).astype(np.float32).astype(dtype).astype(np.float64)
    return np.moveaxis((codes * scale).reshape(v.shape), -1, axis)


WIDE = False


def mx_kscale(k):
    if not WIDE:
        return np.ones(k)
    levels = np.array([20, -20, 10, -10, 0])
    if k % 512:
        return np.exp2(np.random.permutation(np.resize(levels, k // 32))).repeat(32)
    a = np.empty((k // 512, 16))
    for p in range(k // 512):
        a[p, :8] = np.random.permutation(np.resize(levels, 8))
        for g in range(8):
            far = levels[np.abs(levels - a[p, g]) >= 10]
            a[p, g + 8] = far[np.random.randint(len(far))]
    return np.exp2(a.ravel()).repeat(32)


BF16 = ml_dtypes.bfloat16


def bf(x):
    return np.asarray(x, np.float32).astype(BF16)


def f64(x):
    return np.asarray(x).astype(np.float64)


B, T, C, R, H, DN, DR, DV = 2, 256, 512, 512, 16, 32, 32, 128
DQ = DN + DR
NF = DR // 2


def rotate_half(u):
    u1, u2 = u[..., : u.shape[-1] // 2], u[..., u.shape[-1] // 2 :]
    return np.concatenate([-u2, u1], axis=-1)


def setup_inputs():
    u = np.array(mx_kscale(H * DQ), dtype=np.float64).reshape(H, DQ)
    u[:, DN + NF :] = u[:, DN : DN + NF]
    x = np.random.standard_normal((B, T, C))
    freqs_cis = np.stack([np.random.uniform(size=(T, NF)), np.random.uniform(size=(T, NF))], axis=-1)
    w_q = np.random.standard_normal((C, H * DQ)) / np.sqrt(C) / u.reshape(1, H * DQ)
    g = np.random.standard_normal((B, T, H, DQ)) * np.exp2(np.random.randint(-12, 1, (B, T, 1, 1))) * 4.0 * u
    return {"x": bf(x), "freqs_cis": bf(freqs_cis), "w_q": bf(w_q), "grad_out": bf(g)}


def reference(x, freqs_cis, w_q, grad_out):
    g = f64(grad_out)
    freqs = f64(freqs_cis)
    cos = freqs[..., 0][None, :, None, :]
    sin = freqs[..., 1][None, :, None, :]
    g1 = g[..., DN : DN + NF]
    g2 = g[..., DN + NF :]
    gq = np.concatenate([g[..., :DN], g1 * cos + g2 * sin, g2 * cos - g1 * sin], axis=-1).reshape(B, T, H * DQ)
    return mxq(gq, 2, "e5m2") @ mxq(f64(w_q), 1, "e4m3").T

@@ -1,0 +1,139 @@
+from contextlib import ExitStack
+
+import concourse.mybir as mybir
+from concourse.masks import make_identity
+
+BF16 = mybir.dt.bfloat16
+F32 = mybir.dt.float32
+U32 = mybir.dt.uint32
+U8 = mybir.dt.uint8
+E5M2_X4 = mybir.dt.float8_e5m2_x4
+E4M3_X4 = mybir.dt.float8_e4m3fn_x4
+
+P = 128
+POSITIONS = 256
+TOKENS = 512
+HEADS = 16
+HEAD = 64
+PLAIN = 32
+NF = 16
+K = HEADS * HEAD
+C = 512
+PASSES = K // (4 * P)
+BLOCKS = 2
+TOKEN_TILES = TOKENS // P
+POSITION_TILES = POSITIONS // P
+C_TILES = C // P
+
+FLOPS = 2 * TOKENS * C * K
+BYTES = 2 * (TOKENS * K + C * K + POSITIONS * 2 * NF) + 4 * TOKENS * C
+
+
+def k_onto_partitions(nc, psum, stage, identity, rows):
+    words = rows.bitcast(F32)
+    flipped = psum.tile([P, PASSES * BLOCKS, P], F32)
+    for b in range(PASSES * BLOCKS):
+        g, u = divmod(b, BLOCKS)
+        first = g * BLOCKS * P
+        nc.tensor.transpose(flipped[:, b, :], words[:, first + u : first + BLOCKS * P : BLOCKS], identity)
+    grouped = stage.tile([P, PASSES, P, BLOCKS], F32, align_bytes=64)
+    nc.scalar.copy(out=grouped[:], in_=flipped[:].rearrange("p (g u) r -> p g r u", u=BLOCKS))
+    return grouped[:].rearrange("p g r u -> p g (r u)").bitcast(BF16)
+
+
+def tile_fa3mlaattention_pb_s_kernel(tc, x, freqs_cis, w_q, grad_out, out):
+    nc = tc.nc
+    grad_rows = grad_out.rearrange("b t h d -> (b t) (h d)")
+    out_rows = out.rearrange("b t c -> (b t) c")
+
+    with ExitStack() as ctx:
+        keep = ctx.enter_context(tc.tile_pool(name="keep", bufs=1))
+        turn = ctx.enter_context(tc.tile_pool(name="turn", bufs=TOKEN_TILES))
+        stage = ctx.enter_context(tc.tile_pool(name="stage", bufs=TOKEN_TILES + C_TILES))
+        flip_psum = ctx.enter_context(tc.psum_pool(name="flip_psum", bufs=4))
+        acc_psum = ctx.enter_context(tc.psum_pool(name="acc_psum", bufs=TOKEN_TILES))
+        ctx.enter_context(tc.manual_schedule())
+
+        freqs = keep.tile([P, POSITION_TILES, 2 * NF], BF16)
+        nc.sync.dma_start(out=freqs[:], in_=freqs_cis.rearrange("(a p) j c -> p a (j c)", p=P))
+        grads = [keep.tile([P, K], BF16, name="grad%d" % i) for i in range(TOKEN_TILES)]
+        weights = [keep.tile([P, K], BF16, name="weight%d" % j) for j in range(C_TILES)]
+        for first in range(0, TOKEN_TILES, 2):
+            for i in (first, first + 1):
+                nc.sync.dma_start(out=grads[i][:], in_=grad_rows[i * P : (i + 1) * P, :])
+            for j in (first, first + 1):
+                nc.sync.dma_start(out=weights[j][:], in_=w_q[j * P : (j + 1) * P, :])
+
+        identity = keep.tile([P, P], F32)
+        make_identity(nc, identity[:])
+
+        freq_rows = freqs[:].rearrange("p a (j c) -> p a c j", c=2)
+        halves = [
+            g[:].rearrange("p (h d) -> p h d", d=HEAD)[:, :, PLAIN:HEAD].rearrange("p h (s j) -> p h s j", s=2)
+            for g in grads
+        ]
+        by_cos = [turn.tile([P, HEADS, 2, NF], F32, name="by_cos") for g in grads]
+        by_sin = [turn.tile([P, HEADS, 2, NF], F32, name="by_sin") for g in grads]
+        grad_grouped = []
+        weight_grouped = []
+
+        def over_heads(row):
+            return row.unsqueeze(1).unsqueeze(1).to_broadcast([P, HEADS, 2, NF])
+
+        def add_up(i):
+            nc.vector.tensor_add(out=halves[i][:, :, 0, :], in0=by_cos[i][:, :, 0, :], in1=by_sin[i][:, :, 1, :])
+            nc.vector.tensor_sub(out=halves[i][:, :, 1, :], in0=by_cos[i][:, :, 1, :], in1=by_sin[i][:, :, 0, :])
+            grad_grouped.append(k_onto_partitions(nc, flip_psum, stage, identity[:], grads[i][:]))
+
+        for i in range(TOKEN_TILES):
+            a = i % POSITION_TILES
+            nc.vector.tensor_mul(out=by_cos[i][:], in0=halves[i], in1=over_heads(freq_rows[:, a, 0, :]))
+            nc.vector.tensor_mul(out=by_sin[i][:], in0=halves[i], in1=over_heads(freq_rows[:, a, 1, :]))
+            if i > 0:
+                add_up(i - 1)
+            if i % 2 == 0:
+                for j in (i, i + 1):
+                    weight_grouped.append(k_onto_partitions(nc, flip_psum, stage, identity[:], weights[j][:]))
+        add_up(TOKEN_TILES - 1)
+
+        grad_codes = [keep.tile([P, PASSES, P], U32, name="grad_codes%d" % i, align_bytes=64) for i in range(TOKEN_TILES)]
+        grad_scales = [keep.tile([P, PASSES, P], U8, name="grad_scales%d" % i, align_bytes=64) for i in range(TOKEN_TILES)]
+        weight_codes = keep.tile([P, PASSES, C], U32, align_bytes=64)
+        weight_scales = keep.tile([P, PASSES, C], U8, align_bytes=64)
+
+        def quantise_grad(i):
+            nc.vector.quantize_mx(
+                out=grad_codes[i][:].rearrange("p g r -> p (g r)").bitcast(E5M2_X4),
+                scales=grad_scales[i][:].rearrange("p g r -> p (g r)"),
+                in_=grad_grouped[i].rearrange("p g f -> p (g f)"),
+            )
+
+        quantise_grad(0)
+        for g in range(PASSES):
+            for j in range(C_TILES):
+                nc.vector.quantize_mx(
+                    out=weight_codes[:, g, j * P : (j + 1) * P].bitcast(E4M3_X4),
+                    scales=weight_scales[:, g, j * P : (j + 1) * P],
+                    in_=weight_grouped[j][:, g, :],
+                )
+        for i in range(1, TOKEN_TILES):
+            quantise_grad(i)
+
+        for i in range(TOKEN_TILES):
+            acc = acc_psum.tile([P, C], F32)
+            for g in range(PASSES):
+                nc.tensor.matmul_mx(
+                    out=acc[:],
+                    lhsT=grad_codes[i][:, g, :].bitcast(E5M2_X4),
+                    lhsT_scale=grad_scales[i][:, g, :],
+                    rhs=weight_codes[:, g, :].bitcast(E4M3_X4),
+                    rhs_scale=weight_scales[:, g, :],
+                    start=(g == 0),
+                    stop=(g == PASSES - 1),
+                )
+            result = turn.tile([P, C], F32)
+            if i % 2 == 0:
+                nc.scalar.copy(out=result[:], in_=acc[:])
+            else:
+                nc.vector.tensor_copy(out=result[:], in_=acc[:])
+            nc.sync.dma_start(out=out_rows[i * P : (i + 1) * P, :], in_=result[:])

@@ -58,48 +58,66 @@ def tile_fa3mlaattention_pb_s_kernel(tc, x, freqs_cis, w_q, grad_out, out):
         nc.sync.dma_start(out=freqs[:], in_=freqs_cis.rearrange("(a p) j c -> p a (j c)", p=P))
         grads = [keep.tile([P, K], BF16, name="grad%d" % i) for i in range(TOKEN_TILES)]
         weights = [keep.tile([P, K], BF16, name="weight%d" % j) for j in range(C_TILES)]
-        for first in range(0, TOKEN_TILES, 2):
-            for i in (first, first + 1):
-                nc.sync.dma_start(out=grads[i][:], in_=grad_rows[i * P : (i + 1) * P, :])
-            for j in (first, first + 1):
-                nc.sync.dma_start(out=weights[j][:], in_=w_q[j * P : (j + 1) * P, :])
+
+        def load_grad(i):
+            nc.sync.dma_start(out=grads[i][:], in_=grad_rows[i * P : (i + 1) * P, :])
+
+        def load_weight(j):
+            nc.sync.dma_start(out=weights[j][:], in_=w_q[j * P : (j + 1) * P, :])
+
+        load_grad(0)
+        load_weight(0)
+        load_grad(1)
+        load_weight(1)
+        load_grad(2)
+        load_weight(2)
+        load_weight(3)
+        load_grad(3)
 
         identity = keep.tile([P, P], F32)
         make_identity(nc, identity[:])
-
-        freq_rows = freqs[:].rearrange("p a (j c) -> p a c j", c=2)
+        identity_bf16 = keep.tile([P, P], BF16)
+        nc.vector.tensor_copy(out=identity_bf16[:], in_=identity[:])
+        table = acc_psum.tile([P, C], F32, name="acc")
+        pairs = POSITION_TILES * 2 * NF
+        nc.tensor.matmul(
+            table[:, :pairs],
+            lhsT=identity_bf16[:],
+            rhs=freqs[:].rearrange("p a x -> p (a x)"),
+            start=True,
+            stop=True,
+        )
+        freq_rows = table[:, :pairs].rearrange("p (a j c) -> p a c j", a=POSITION_TILES, c=2)
         halves = [
             g[:].rearrange("p (h d) -> p h d", d=HEAD)[:, :, PLAIN:HEAD].rearrange("p h (s j) -> p h s j", s=2)
             for g in grads
         ]
         by_cos = [turn.tile([P, HEADS, 2, NF], F32, name="by_cos") for g in grads]
         by_sin = [turn.tile([P, HEADS, 2, NF], F32, name="by_sin") for g in grads]
-        grad_grouped = []
-        weight_grouped = []
-
-        def over_heads(row):
-            return row.unsqueeze(1).unsqueeze(1).to_broadcast([P, HEADS, 2, NF])
-
-        def add_up(i):
-            nc.vector.tensor_add(out=halves[i][:, :, 0, :], in0=by_cos[i][:, :, 0, :], in1=by_sin[i][:, :, 1, :])
-            nc.vector.tensor_sub(out=halves[i][:, :, 1, :], in0=by_cos[i][:, :, 1, :], in1=by_sin[i][:, :, 0, :])
-            grad_grouped.append(k_onto_partitions(nc, flip_psum, stage, identity[:], grads[i][:]))
-
-        for i in range(TOKEN_TILES):
-            a = i % POSITION_TILES
-            nc.vector.tensor_mul(out=by_cos[i][:], in0=halves[i], in1=over_heads(freq_rows[:, a, 0, :]))
-            nc.vector.tensor_mul(out=by_sin[i][:], in0=halves[i], in1=over_heads(freq_rows[:, a, 1, :]))
-            if i > 0:
-                add_up(i - 1)
-            if i % 2 == 0:
-                for j in (i, i + 1):
-                    weight_grouped.append(k_onto_partitions(nc, flip_psum, stage, identity[:], weights[j][:]))
-        add_up(TOKEN_TILES - 1)
-
         grad_codes = [keep.tile([P, PASSES, P], U32, name="grad_codes%d" % i, align_bytes=64) for i in range(TOKEN_TILES)]
         grad_scales = [keep.tile([P, PASSES, P], U8, name="grad_scales%d" % i, align_bytes=64) for i in range(TOKEN_TILES)]
         weight_codes = keep.tile([P, PASSES, C], U32, align_bytes=64)
         weight_scales = keep.tile([P, PASSES, C], U8, align_bytes=64)
+        grad_grouped = {}
+        weight_grouped = {}
+
+        def over_heads(row):
+            return row.unsqueeze(1).unsqueeze(1).to_broadcast([P, HEADS, 2, NF])
+
+        def products(i):
+            a = i % POSITION_TILES
+            nc.vector.tensor_mul(out=by_cos[i][:], in0=halves[i], in1=over_heads(freq_rows[:, a, 0, :]))
+            nc.vector.tensor_mul(out=by_sin[i][:], in0=halves[i], in1=over_heads(freq_rows[:, a, 1, :]))
+
+        def sums(engine, i):
+            engine.tensor_add(out=halves[i][:, :, 0, :], in0=by_cos[i][:, :, 0, :], in1=by_sin[i][:, :, 1, :])
+            engine.tensor_sub(out=halves[i][:, :, 1, :], in0=by_cos[i][:, :, 1, :], in1=by_sin[i][:, :, 0, :])
+
+        def flip_grad(i):
+            grad_grouped[i] = k_onto_partitions(nc, flip_psum, stage, identity[:], grads[i][:])
+
+        def flip_weight(j):
+            weight_grouped[j] = k_onto_partitions(nc, flip_psum, stage, identity[:], weights[j][:])
 
         def quantise_grad(i):
             nc.vector.quantize_mx(
@@ -108,19 +126,41 @@ def tile_fa3mlaattention_pb_s_kernel(tc, x, freqs_cis, w_q, grad_out, out):
                 in_=grad_grouped[i].rearrange("p g f -> p (g f)"),
             )
 
-        quantise_grad(0)
-        for g in range(PASSES):
-            for j in range(C_TILES):
+        def quantise_weight(j):
+            for g in range(PASSES):
                 nc.vector.quantize_mx(
                     out=weight_codes[:, g, j * P : (j + 1) * P].bitcast(E4M3_X4),
                     scales=weight_scales[:, g, j * P : (j + 1) * P],
                     in_=weight_grouped[j][:, g, :],
                 )
-        for i in range(1, TOKEN_TILES):
-            quantise_grad(i)
+
+        products(0)
+        flip_weight(0)
+        sums(nc.gpsimd, 0)
+        products(1)
+        flip_weight(1)
+        sums(nc.gpsimd, 1)
+        quantise_weight(0)
+        products(2)
+        flip_weight(2)
+        sums(nc.gpsimd, 2)
+        flip_grad(0)
+        flip_weight(3)
+        quantise_weight(1)
+        products(3)
+        quantise_weight(2)
+        sums(nc.vector, 3)
+        flip_grad(1)
+        quantise_grad(0)
+        quantise_weight(3)
+        flip_grad(2)
+        quantise_grad(1)
+        flip_grad(3)
+        quantise_grad(2)
+        quantise_grad(3)
 
         for i in range(TOKEN_TILES):
-            acc = acc_psum.tile([P, C], F32)
+            acc = acc_psum.tile([P, C], F32, name="acc")
             for g in range(PASSES):
                 nc.tensor.matmul_mx(
                     out=acc[:],
@@ -132,8 +172,5 @@ def tile_fa3mlaattention_pb_s_kernel(tc, x, freqs_cis, w_q, grad_out, out):
                     stop=(g == PASSES - 1),
                 )
             result = turn.tile([P, C], F32)
-            if i % 2 == 0:
-                nc.scalar.copy(out=result[:], in_=acc[:])
-            else:
-                nc.vector.tensor_copy(out=result[:], in_=acc[:])
+            nc.scalar.copy(out=result[:], in_=acc[:])
             nc.sync.dma_start(out=out_rows[i * P : (i + 1) * P, :], in_=result[:])

@@ -66,16 +66,23 @@ def tile_fa3mlaattention_pb_s_kernel(tc, x, freqs_cis, w_q, grad_out, out):
             nc.sync.dma_start(out=weights[j][:], in_=w_q[j * P : (j + 1) * P, :])
 
         load_grad(0)
-        load_weight(0)
         load_grad(1)
-        load_weight(1)
+        load_weight(0)
         load_grad(2)
+        load_weight(1)
+        load_grad(3)
         load_weight(2)
         load_weight(3)
-        load_grad(3)
 
         identity = keep.tile([P, P], F32)
         make_identity(nc, identity[:])
+        warm = acc_psum.tile([P, C], F32, name="acc")
+
+        def keep_warm(times):
+            for turn_number in range(times):
+                nc.tensor.matmul(warm[:, :P], lhsT=identity[:], rhs=identity[:], start=True, stop=True)
+
+        keep_warm(5)
         identity_bf16 = keep.tile([P, P], BF16)
         nc.vector.tensor_copy(out=identity_bf16[:], in_=identity[:])
         table = acc_psum.tile([P, C], F32, name="acc")
@@ -135,29 +142,33 @@ def tile_fa3mlaattention_pb_s_kernel(tc, x, freqs_cis, w_q, grad_out, out):
                 )
 
         products(0)
-        flip_weight(0)
-        sums(nc.gpsimd, 0)
         products(1)
-        flip_weight(1)
-        sums(nc.gpsimd, 1)
-        quantise_weight(0)
         products(2)
-        flip_weight(2)
-        sums(nc.gpsimd, 2)
-        flip_grad(0)
-        flip_weight(3)
-        quantise_weight(1)
         products(3)
-        quantise_weight(2)
-        sums(nc.vector, 3)
+        sums(nc.gpsimd, 0)
+        sums(nc.gpsimd, 1)
+        flip_weight(0)
+        keep_warm(2)
+        flip_weight(1)
+        keep_warm(1)
+        flip_grad(0)
+        flip_weight(2)
+        flip_weight(3)
         flip_grad(1)
-        quantise_grad(0)
-        quantise_weight(3)
+        keep_warm(1)
+        sums(nc.vector, 2)
+        quantise_weight(0)
+        sums(nc.vector, 3)
         flip_grad(2)
-        quantise_grad(1)
+        keep_warm(1)
         flip_grad(3)
-        quantise_grad(2)
-        quantise_grad(3)
+        keep_warm(2)
+        quantise_weight(1)
+        quantise_grad(0)
+        quantise_weight(2)
+        quantise_weight(3)
+        for i in range(1, TOKEN_TILES):
+            quantise_grad(i)
 
         for i in range(TOKEN_TILES):
             acc = acc_psum.tile([P, C], F32, name="acc")

@@ -29,16 +29,19 @@ FLOPS = 2 * TOKENS * C * K
 BYTES = 2 * (TOKENS * K + C * K + POSITIONS * 2 * NF) + 4 * TOKENS * C
 
 
-def k_onto_partitions(nc, psum, stage, identity, rows):
+def k_onto_partitions(nc, psum, grouped, identity, rows, passes):
     words = rows.bitcast(F32)
     flipped = psum.tile([P, PASSES * BLOCKS, P], F32)
-    for b in range(PASSES * BLOCKS):
-        g, u = divmod(b, BLOCKS)
-        first = g * BLOCKS * P
-        nc.tensor.transpose(flipped[:, b, :], words[:, first + u : first + BLOCKS * P : BLOCKS], identity)
-    grouped = stage.tile([P, PASSES, P, BLOCKS], F32, align_bytes=64)
-    nc.scalar.copy(out=grouped[:], in_=flipped[:].rearrange("p (g u) r -> p g r u", u=BLOCKS))
-    return grouped[:].rearrange("p g r u -> p g (r u)").bitcast(BF16)
+    for at, g in enumerate(passes):
+        for u in range(BLOCKS):
+            first = g * BLOCKS * P
+            nc.tensor.transpose(
+                flipped[:, at * BLOCKS + u, :], words[:, first + u : first + BLOCKS * P : BLOCKS], identity
+            )
+    nc.scalar.copy(
+        out=grouped[:, passes[0] : passes[-1] + 1],
+        in_=flipped[:, : len(passes) * BLOCKS].rearrange("p (g u) r -> p g r u", u=BLOCKS),
+    )
 
 
 def tile_fa3mlaattention_pb_s_kernel(tc, x, freqs_cis, w_q, grad_out, out):
@@ -82,19 +85,19 @@ def tile_fa3mlaattention_pb_s_kernel(tc, x, freqs_cis, w_q, grad_out, out):
             for turn_number in range(times):
                 nc.tensor.matmul(warm[:, :P], lhsT=identity[:], rhs=identity[:], start=True, stop=True)
 
-        keep_warm(5)
+        keep_warm(2)
         identity_bf16 = keep.tile([P, P], BF16)
         nc.vector.tensor_copy(out=identity_bf16[:], in_=identity[:])
+        minus_identity = keep.tile([P, P], BF16)
+        nc.vector.tensor_scalar_mul(out=minus_identity[:], in0=identity[:], scalar1=-1.0)
         table = acc_psum.tile([P, C], F32, name="acc")
-        pairs = POSITION_TILES * 2 * NF
+        angles = POSITION_TILES * NF
+        pairs = freqs[:].rearrange("p a (j c) -> p c (a j)", c=2)
+        nc.tensor.matmul(table[:, : 2 * angles], lhsT=identity_bf16[:], rhs=pairs, start=True, stop=True)
         nc.tensor.matmul(
-            table[:, :pairs],
-            lhsT=identity_bf16[:],
-            rhs=freqs[:].rearrange("p a x -> p (a x)"),
-            start=True,
-            stop=True,
+            table[:, 2 * angles : 3 * angles], lhsT=minus_identity[:], rhs=pairs[:, 1, :], start=True, stop=True
         )
-        freq_rows = table[:, :pairs].rearrange("p (a j c) -> p a c j", a=POSITION_TILES, c=2)
+        table_rows = table[:, : 3 * angles].rearrange("p (c a j) -> p c a j", c=3, a=POSITION_TILES)
         halves = [
             g[:].rearrange("p (h d) -> p h d", d=HEAD)[:, :, PLAIN:HEAD].rearrange("p h (s j) -> p h s j", s=2)
             for g in grads
@@ -105,32 +108,41 @@ def tile_fa3mlaattention_pb_s_kernel(tc, x, freqs_cis, w_q, grad_out, out):
         grad_scales = [keep.tile([P, PASSES, P], U8, name="grad_scales%d" % i, align_bytes=64) for i in range(TOKEN_TILES)]
         weight_codes = keep.tile([P, PASSES, C], U32, align_bytes=64)
         weight_scales = keep.tile([P, PASSES, C], U8, align_bytes=64)
-        grad_grouped = {}
-        weight_grouped = {}
+        both_passes = list(range(PASSES))
+        grad_grouped = [stage.tile([P, PASSES, P, BLOCKS], F32, name="grouped", align_bytes=64) for g in grads]
+        weight_grouped = [stage.tile([P, PASSES, P, BLOCKS], F32, name="grouped", align_bytes=64) for w in weights]
 
-        def over_heads(row):
-            return row.unsqueeze(1).unsqueeze(1).to_broadcast([P, HEADS, 2, NF])
+        def cosines(i):
+            row = table_rows[:, 0, i % POSITION_TILES, :]
+            nc.vector.tensor_mul(
+                out=by_cos[i][:],
+                in0=halves[i],
+                in1=row.unsqueeze(1).unsqueeze(1).to_broadcast([P, HEADS, 2, NF]),
+            )
 
-        def products(i):
-            a = i % POSITION_TILES
-            nc.vector.tensor_mul(out=by_cos[i][:], in0=halves[i], in1=over_heads(freq_rows[:, a, 0, :]))
-            nc.vector.tensor_mul(out=by_sin[i][:], in0=halves[i], in1=over_heads(freq_rows[:, a, 1, :]))
+        def sines(i):
+            rows = table_rows[:, 1:3, i % POSITION_TILES, :]
+            nc.vector.tensor_mul(
+                out=by_sin[i][:],
+                in0=halves[i][:, :, ::-1, :],
+                in1=rows.unsqueeze(1).to_broadcast([P, HEADS, 2, NF]),
+            )
 
         def sums(engine, i):
-            engine.tensor_add(out=halves[i][:, :, 0, :], in0=by_cos[i][:, :, 0, :], in1=by_sin[i][:, :, 1, :])
-            engine.tensor_sub(out=halves[i][:, :, 1, :], in0=by_cos[i][:, :, 1, :], in1=by_sin[i][:, :, 0, :])
+            engine.tensor_add(out=halves[i], in0=by_cos[i][:], in1=by_sin[i][:])
 
-        def flip_grad(i):
-            grad_grouped[i] = k_onto_partitions(nc, flip_psum, stage, identity[:], grads[i][:])
+        def flip_grad(i, passes):
+            k_onto_partitions(nc, flip_psum, grad_grouped[i], identity[:], grads[i][:], passes)
 
         def flip_weight(j):
-            weight_grouped[j] = k_onto_partitions(nc, flip_psum, stage, identity[:], weights[j][:])
+            k_onto_partitions(nc, flip_psum, weight_grouped[j], identity[:], weights[j][:], both_passes)
 
-        def quantise_grad(i):
+        def quantise_grad(i, passes):
+            chosen = slice(passes[0], passes[-1] + 1)
             nc.vector.quantize_mx(
-                out=grad_codes[i][:].rearrange("p g r -> p (g r)").bitcast(E5M2_X4),
-                scales=grad_scales[i][:].rearrange("p g r -> p (g r)"),
-                in_=grad_grouped[i].rearrange("p g f -> p (g f)"),
+                out=grad_codes[i][:, chosen].rearrange("p g r -> p (g r)").bitcast(E5M2_X4),
+                scales=grad_scales[i][:, chosen].rearrange("p g r -> p (g r)"),
+                in_=grad_grouped[i][:, chosen].rearrange("p g r u -> p (g r u)").bitcast(BF16),
             )
 
         def quantise_weight(j):
@@ -138,39 +150,41 @@ def tile_fa3mlaattention_pb_s_kernel(tc, x, freqs_cis, w_q, grad_out, out):
                 nc.vector.quantize_mx(
                     out=weight_codes[:, g, j * P : (j + 1) * P].bitcast(E4M3_X4),
                     scales=weight_scales[:, g, j * P : (j + 1) * P],
-                    in_=weight_grouped[j][:, g, :],
+                    in_=weight_grouped[j][:, g].rearrange("p r u -> p (r u)").bitcast(BF16),
                 )
 
-        products(0)
-        products(1)
-        products(2)
-        products(3)
-        sums(nc.gpsimd, 0)
-        sums(nc.gpsimd, 1)
+        keep_warm(3)
+        for i in range(TOKEN_TILES):
+            cosines(i)
+            sines(i)
+        for i in range(TOKEN_TILES - 1):
+            sums(nc.gpsimd, i)
         flip_weight(0)
         keep_warm(2)
         flip_weight(1)
         keep_warm(1)
-        flip_grad(0)
+        flip_grad(0, both_passes)
+        keep_warm(1)
         flip_weight(2)
         flip_weight(3)
-        flip_grad(1)
+        flip_grad(1, both_passes)
         keep_warm(1)
-        sums(nc.vector, 2)
         quantise_weight(0)
         sums(nc.vector, 3)
-        flip_grad(2)
+        flip_grad(3, both_passes)
+        for g in range(PASSES):
+            flip_grad(2, [g])
         keep_warm(1)
-        flip_grad(3)
-        keep_warm(2)
-        quantise_weight(1)
-        quantise_grad(0)
-        quantise_weight(2)
-        quantise_weight(3)
-        for i in range(1, TOKEN_TILES):
-            quantise_grad(i)
+        for j in range(1, C_TILES - 1):
+            quantise_weight(j)
+        quantise_grad(0, both_passes)
+        quantise_weight(C_TILES - 1)
+        quantise_grad(1, both_passes)
+        quantise_grad(3, both_passes)
+        for g in range(PASSES):
+            quantise_grad(2, [g])
 
-        for i in range(TOKEN_TILES):
+        for i in (0, 1, 3, 2):
             acc = acc_psum.tile([P, C], F32, name="acc")
             for g in range(PASSES):
                 nc.tensor.matmul_mx(
@@ -183,5 +197,8 @@ def tile_fa3mlaattention_pb_s_kernel(tc, x, freqs_cis, w_q, grad_out, out):
                     stop=(g == PASSES - 1),
                 )
             result = turn.tile([P, C], F32)
-            nc.scalar.copy(out=result[:], in_=acc[:])
-            nc.sync.dma_start(out=out_rows[i * P : (i + 1) * P, :], in_=result[:])
+            parts = 2 if i == 2 else 1
+            for part in range(parts):
+                columns = slice(part * C // parts, (part + 1) * C // parts)
+                nc.scalar.copy(out=result[:, columns], in_=acc[:, columns])
+                nc.sync.dma_start(out=out_rows[i * P : (i + 1) * P, columns], in_=result[:, columns])

@@ -160,18 +160,20 @@ def tile_fa3mlaattention_pb_s_kernel(tc, x, freqs_cis, w_q, grad_out, out):
         for i in range(TOKEN_TILES - 1):
             sums(nc.gpsimd, i)
         flip_weight(0)
-        keep_warm(2)
+        keep_warm(1)
         flip_weight(1)
         keep_warm(1)
         flip_grad(0, both_passes)
         keep_warm(1)
         flip_weight(2)
         flip_weight(3)
+        keep_warm(1)
         flip_grad(1, both_passes)
         keep_warm(1)
         quantise_weight(0)
         sums(nc.vector, 3)
         flip_grad(3, both_passes)
+        keep_warm(1)
         for g in range(PASSES):
             flip_grad(2, [g])
         keep_warm(1)

@@ -24,6 +24,7 @@ BLOCKS = 2
 TOKEN_TILES = TOKENS // P
 POSITION_TILES = POSITIONS // P
 C_TILES = C // P
+PAIR = 2
 
 FLOPS = 2 * TOKENS * C * K
 BYTES = 2 * (TOKENS * K + C * K + POSITIONS * 2 * NF) + 4 * TOKENS * C
@@ -62,18 +63,19 @@ def tile_fa3mlaattention_pb_s_kernel(tc, x, freqs_cis, w_q, grad_out, out):
         grads = [keep.tile([P, K], BF16, name="grad%d" % i) for i in range(TOKEN_TILES)]
         weights = [keep.tile([P, K], BF16, name="weight%d" % j) for j in range(C_TILES)]
 
-        def load_grad(i):
-            nc.sync.dma_start(out=grads[i][:], in_=grad_rows[i * P : (i + 1) * P, :])
+        def load_grad(i, columns):
+            nc.sync.dma_start(out=grads[i][:, columns], in_=grad_rows[i * P : (i + 1) * P, columns])
 
         def load_weight(j):
             nc.sync.dma_start(out=weights[j][:], in_=w_q[j * P : (j + 1) * P, :])
 
-        load_grad(0)
-        load_grad(1)
+        load_grad(0, slice(0, K // 2))
+        load_grad(0, slice(K // 2, K))
+        load_grad(1, slice(0, K))
         load_weight(0)
-        load_grad(2)
+        load_grad(2, slice(0, K))
         load_weight(1)
-        load_grad(3)
+        load_grad(3, slice(0, K))
         load_weight(2)
         load_weight(3)
 
@@ -110,14 +112,18 @@ def tile_fa3mlaattention_pb_s_kernel(tc, x, freqs_cis, w_q, grad_out, out):
         weight_scales = keep.tile([P, PASSES, C], U8, align_bytes=64)
         both_passes = list(range(PASSES))
         grad_grouped = [stage.tile([P, PASSES, P, BLOCKS], F32, name="grouped", align_bytes=64) for g in grads]
-        weight_grouped = [stage.tile([P, PASSES, P, BLOCKS], F32, name="grouped", align_bytes=64) for w in weights]
+        weight_grouped = [
+            keep.tile([P, PASSES, PAIR * P, BLOCKS], F32, name="weight_grouped%d" % pair, align_bytes=64)
+            for pair in range(C_TILES // PAIR)
+        ]
 
-        def cosines(i):
+        def cosines(i, heads):
             row = table_rows[:, 0, i % POSITION_TILES, :]
+            chosen = halves[i][:, heads]
             nc.vector.tensor_mul(
-                out=by_cos[i][:],
-                in0=halves[i],
-                in1=row.unsqueeze(1).unsqueeze(1).to_broadcast([P, HEADS, 2, NF]),
+                out=by_cos[i][:, heads],
+                in0=chosen,
+                in1=row.unsqueeze(1).unsqueeze(1).to_broadcast(list(chosen.shape)),
             )
 
         def sines(i):
@@ -128,14 +134,29 @@ def tile_fa3mlaattention_pb_s_kernel(tc, x, freqs_cis, w_q, grad_out, out):
                 in1=rows.unsqueeze(1).to_broadcast([P, HEADS, 2, NF]),
             )
 
+        def first_sines():
+            sin_row = freqs[:].rearrange("p a (j c) -> p a c j", c=2)[:, 0, 1, :]
+            nc.gpsimd.tensor_mul(
+                out=by_sin[0][:, :, 0, :],
+                in0=halves[0][:, :, 1, :],
+                in1=sin_row.unsqueeze(1).to_broadcast([P, HEADS, NF]),
+            )
+            nc.vector.tensor_mul(
+                out=by_sin[0][:, :, 1, :],
+                in0=halves[0][:, :, 0, :],
+                in1=table_rows[:, 2, 0, :].unsqueeze(1).to_broadcast([P, HEADS, NF]),
+            )
+
         def sums(engine, i):
             engine.tensor_add(out=halves[i], in0=by_cos[i][:], in1=by_sin[i][:])
 
         def flip_grad(i, passes):
-            k_onto_partitions(nc, flip_psum, grad_grouped[i], identity[:], grads[i][:], passes)
+            k_onto_partitions(nc, flip_psum, grad_grouped[i][:], identity[:], grads[i][:], passes)
 
         def flip_weight(j):
-            k_onto_partitions(nc, flip_psum, weight_grouped[j], identity[:], weights[j][:], both_passes)
+            pair, member = divmod(j, PAIR)
+            grouped = weight_grouped[pair][:, :, member * P : (member + 1) * P, :]
+            k_onto_partitions(nc, flip_psum, grouped, identity[:], weights[j][:], both_passes)
 
         def quantise_grad(i, passes):
             chosen = slice(passes[0], passes[-1] + 1)
@@ -145,48 +166,49 @@ def tile_fa3mlaattention_pb_s_kernel(tc, x, freqs_cis, w_q, grad_out, out):
                 in_=grad_grouped[i][:, chosen].rearrange("p g r u -> p (g r u)").bitcast(BF16),
             )
 
-        def quantise_weight(j):
+        def quantise_weights(pair):
+            columns = slice(pair * PAIR * P, (pair + 1) * PAIR * P)
             for g in range(PASSES):
                 nc.vector.quantize_mx(
-                    out=weight_codes[:, g, j * P : (j + 1) * P].bitcast(E4M3_X4),
-                    scales=weight_scales[:, g, j * P : (j + 1) * P],
-                    in_=weight_grouped[j][:, g].rearrange("p r u -> p (r u)").bitcast(BF16),
+                    out=weight_codes[:, g, columns].bitcast(E4M3_X4),
+                    scales=weight_scales[:, g, columns],
+                    in_=weight_grouped[pair][:, g].rearrange("p r u -> p (r u)").bitcast(BF16),
                 )
 
         keep_warm(3)
-        for i in range(TOKEN_TILES):
-            cosines(i)
+        cosines(0, slice(0, HEADS // 2))
+        cosines(0, slice(HEADS // 2, HEADS))
+        first_sines()
+        for i in range(1, TOKEN_TILES):
+            cosines(i, slice(0, HEADS))
             sines(i)
-        for i in range(TOKEN_TILES - 1):
-            sums(nc.gpsimd, i)
+        sums(nc.gpsimd, 0)
+        sums(nc.gpsimd, 1)
         flip_weight(0)
         keep_warm(1)
         flip_weight(1)
         keep_warm(1)
         flip_grad(0, both_passes)
-        keep_warm(1)
         flip_weight(2)
-        flip_weight(3)
         keep_warm(1)
         flip_grad(1, both_passes)
+        flip_weight(3)
         keep_warm(1)
-        quantise_weight(0)
+        sums(nc.vector, 2)
         sums(nc.vector, 3)
-        flip_grad(3, both_passes)
+        flip_grad(2, both_passes)
         keep_warm(1)
         for g in range(PASSES):
-            flip_grad(2, [g])
-        keep_warm(1)
-        for j in range(1, C_TILES - 1):
-            quantise_weight(j)
+            flip_grad(3, [g])
+        quantise_weights(0)
         quantise_grad(0, both_passes)
-        quantise_weight(C_TILES - 1)
+        quantise_weights(1)
         quantise_grad(1, both_passes)
-        quantise_grad(3, both_passes)
+        quantise_grad(2, both_passes)
         for g in range(PASSES):
-            quantise_grad(2, [g])
+            quantise_grad(3, [g])
 
-        for i in (0, 1, 3, 2):
+        for i in range(TOKEN_TILES):
             acc = acc_psum.tile([P, C], F32, name="acc")
             for g in range(PASSES):
                 nc.tensor.matmul_mx(
@@ -199,7 +221,7 @@ def tile_fa3mlaattention_pb_s_kernel(tc, x, freqs_cis, w_q, grad_out, out):
                     stop=(g == PASSES - 1),
                 )
             result = turn.tile([P, C], F32)
-            parts = 2 if i == 2 else 1
+            parts = 2 if i == TOKEN_TILES - 1 else 1
             for part in range(parts):
                 columns = slice(part * C // parts, (part + 1) * C // parts)
                 nc.scalar.copy(out=result[:, columns], in_=acc[:, columns])

@@ -30,15 +30,11 @@ FLOPS = 2 * TOKENS * C * K
 BYTES = 2 * (TOKENS * K + C * K + POSITIONS * 2 * NF) + 4 * TOKENS * C
 
 
-def k_onto_partitions(nc, psum, grouped, identity, rows, passes):
-    words = rows.bitcast(F32)
+def k_onto_partitions(nc, psum, grouped, identity, block, passes):
     flipped = psum.tile([P, PASSES * BLOCKS, P], F32)
     for at, g in enumerate(passes):
         for u in range(BLOCKS):
-            first = g * BLOCKS * P
-            nc.tensor.transpose(
-                flipped[:, at * BLOCKS + u, :], words[:, first + u : first + BLOCKS * P : BLOCKS], identity
-            )
+            nc.tensor.transpose(flipped[:, at * BLOCKS + u, :], block(g, u), identity)
     nc.scalar.copy(
         out=grouped[:, passes[0] : passes[-1] + 1],
         in_=flipped[:, : len(passes) * BLOCKS].rearrange("p (g u) r -> p g r u", u=BLOCKS),
@@ -47,8 +43,8 @@ def k_onto_partitions(nc, psum, grouped, identity, rows, passes):
 
 def tile_fa3mlaattention_pb_s_kernel(tc, x, freqs_cis, w_q, grad_out, out):
     nc = tc.nc
-    grad_rows = grad_out.rearrange("b t h d -> (b t) (h d)")
-    out_rows = out.rearrange("b t c -> (b t) c")
+    grad_rows = grad_out.rearrange("b (p a) h d -> b a p (h d)", a=POSITION_TILES)
+    out_rows = out.rearrange("b (p a) c -> b a p c", a=POSITION_TILES)
 
     with ExitStack() as ctx:
         keep = ctx.enter_context(tc.tile_pool(name="keep", bufs=1))
@@ -59,12 +55,12 @@ def tile_fa3mlaattention_pb_s_kernel(tc, x, freqs_cis, w_q, grad_out, out):
         ctx.enter_context(tc.manual_schedule())
 
         freqs = keep.tile([P, POSITION_TILES, 2 * NF], BF16)
-        nc.sync.dma_start(out=freqs[:], in_=freqs_cis.rearrange("(a p) j c -> p a (j c)", p=P))
+        nc.scalar.dma_start(out=freqs[:], in_=freqs_cis.rearrange("(p a) j c -> p a (j c)", a=POSITION_TILES))
         grads = [keep.tile([P, K], BF16, name="grad%d" % i) for i in range(TOKEN_TILES)]
         weights = [keep.tile([P, K], BF16, name="weight%d" % j) for j in range(C_TILES)]
 
         def load_grad(i, columns):
-            nc.sync.dma_start(out=grads[i][:, columns], in_=grad_rows[i * P : (i + 1) * P, columns])
+            nc.sync.dma_start(out=grads[i][:, columns], in_=grad_rows[i // POSITION_TILES, i % POSITION_TILES, :, columns])
 
         def load_weight(j):
             nc.sync.dma_start(out=weights[j][:], in_=w_q[j * P : (j + 1) * P, :])
@@ -78,6 +74,11 @@ def tile_fa3mlaattention_pb_s_kernel(tc, x, freqs_cis, w_q, grad_out, out):
         load_grad(3, slice(0, K))
         load_weight(2)
         load_weight(3)
+
+        blank = keep.tile([P, 1], F32)
+        nc.vector.memset(blank[:], 0.0)
+        blank_copy = keep.tile([P, 1], F32)
+        nc.scalar.copy(out=blank_copy[:], in_=blank[:])
 
         identity = keep.tile([P, P], F32)
         make_identity(nc, identity[:])
@@ -93,19 +94,16 @@ def tile_fa3mlaattention_pb_s_kernel(tc, x, freqs_cis, w_q, grad_out, out):
         minus_identity = keep.tile([P, P], BF16)
         nc.vector.tensor_scalar_mul(out=minus_identity[:], in0=identity[:], scalar1=-1.0)
         table = acc_psum.tile([P, C], F32, name="acc")
-        angles = POSITION_TILES * NF
-        pairs = freqs[:].rearrange("p a (j c) -> p c (a j)", c=2)
-        nc.tensor.matmul(table[:, : 2 * angles], lhsT=identity_bf16[:], rhs=pairs, start=True, stop=True)
-        nc.tensor.matmul(
-            table[:, 2 * angles : 3 * angles], lhsT=minus_identity[:], rhs=pairs[:, 1, :], start=True, stop=True
+        table_rows = table[:, : 4 * POSITION_TILES * NF].rearrange(
+            "p (c a s j) -> p c a s j", c=2, a=POSITION_TILES, s=2
         )
-        table_rows = table[:, : 3 * angles].rearrange("p (c a j) -> p c a j", c=3, a=POSITION_TILES)
-        halves = [
-            g[:].rearrange("p (h d) -> p h d", d=HEAD)[:, :, PLAIN:HEAD].rearrange("p h (s j) -> p h s j", s=2)
-            for g in grads
-        ]
-        by_cos = [turn.tile([P, HEADS, 2, NF], F32, name="by_cos") for g in grads]
-        by_sin = [turn.tile([P, HEADS, 2, NF], F32, name="by_sin") for g in grads]
+        pairs = freqs[:].rearrange("p a (j c) -> p c a j", c=2)
+        for c, s, sign in ((0, 0, identity_bf16), (0, 1, identity_bf16), (1, 1, identity_bf16), (1, 0, minus_identity)):
+            nc.tensor.matmul(table_rows[:, c, :, s, :], lhsT=sign[:], rhs=pairs[:, c], start=True, stop=True)
+
+        gq = [keep.tile([P, BLOCKS, PASSES * P * 2], BF16, name="gq%d" % i) for i in range(TOKEN_TILES)]
+        by_cos = [turn.tile([P, BLOCKS, HEADS, NF], F32, name="by_cos") for i in range(TOKEN_TILES)]
+        by_sin = [turn.tile([P, BLOCKS, HEADS, NF], F32, name="by_sin") for i in range(TOKEN_TILES)]
         grad_codes = [keep.tile([P, PASSES, P], U32, name="grad_codes%d" % i, align_bytes=64) for i in range(TOKEN_TILES)]
         grad_scales = [keep.tile([P, PASSES, P], U8, name="grad_scales%d" % i, align_bytes=64) for i in range(TOKEN_TILES)]
         weight_codes = keep.tile([P, PASSES, C], U32, align_bytes=64)
@@ -117,46 +115,50 @@ def tile_fa3mlaattention_pb_s_kernel(tc, x, freqs_cis, w_q, grad_out, out):
             for pair in range(C_TILES // PAIR)
         ]
 
-        def cosines(i, heads):
-            row = table_rows[:, 0, i % POSITION_TILES, :]
-            chosen = halves[i][:, heads]
+        def products(i, c, into, heads):
+            rotated = grads[i][:].rearrange("p (h d) -> p h d", d=HEAD)[:, heads, PLAIN:HEAD]
+            row = table_rows[:, c, i % POSITION_TILES].rearrange("p s j -> p (s j)")
+            row = row.rearrange("p (x u e) -> p x u e", u=BLOCKS, e=2)
+            chosen = rotated.rearrange("p h (x u e) -> p h x u e", u=BLOCKS, e=2)
             nc.vector.tensor_mul(
-                out=by_cos[i][:, heads],
+                out=into[i][:, :, heads].rearrange("p u h (x e) -> p h x u e", e=2),
                 in0=chosen,
-                in1=row.unsqueeze(1).unsqueeze(1).to_broadcast(list(chosen.shape)),
-            )
-
-        def sines(i):
-            rows = table_rows[:, 1:3, i % POSITION_TILES, :]
-            nc.vector.tensor_mul(
-                out=by_sin[i][:],
-                in0=halves[i][:, :, ::-1, :],
-                in1=rows.unsqueeze(1).to_broadcast([P, HEADS, 2, NF]),
-            )
-
-        def first_sines():
-            sin_row = freqs[:].rearrange("p a (j c) -> p a c j", c=2)[:, 0, 1, :]
-            nc.gpsimd.tensor_mul(
-                out=by_sin[0][:, :, 0, :],
-                in0=halves[0][:, :, 1, :],
-                in1=sin_row.unsqueeze(1).to_broadcast([P, HEADS, NF]),
-            )
-            nc.vector.tensor_mul(
-                out=by_sin[0][:, :, 1, :],
-                in0=halves[0][:, :, 0, :],
-                in1=table_rows[:, 2, 0, :].unsqueeze(1).to_broadcast([P, HEADS, NF]),
+                in1=row.unsqueeze(1).to_broadcast(list(chosen.shape)),
             )
 
         def sums(engine, i):
-            engine.tensor_add(out=halves[i], in0=by_cos[i][:], in1=by_sin[i][:])
+            out_words = gq[i][:].rearrange("p u (h y) -> p u h y", h=HEADS)[:, :, :, NF : 2 * NF]
+            engine.tensor_add(
+                out=out_words.rearrange("p u h (s y) -> p u h s y", s=2),
+                in0=by_cos[i][:].rearrange("p u h (s y) -> p u h s y", s=2),
+                in1=by_sin[i][:].rearrange("p u h (s y) -> p u h s y", s=2)[:, :, :, ::-1, :],
+            )
+
+        def move_plain(i):
+            out_words = gq[i][:].rearrange("p u w -> p (u w)").bitcast(F32)
+            nc.scalar.copy(
+                out=out_words.rearrange("p (u h x) -> p h x u", u=BLOCKS, h=HEADS)[:, :, 0 : NF // 2, :],
+                in_=grads[i][:].bitcast(F32).rearrange("p (h x u) -> p h x u", h=HEADS, u=BLOCKS)[:, :, 0 : NF // 2, :],
+            )
 
         def flip_grad(i, passes):
-            k_onto_partitions(nc, flip_psum, grad_grouped[i][:], identity[:], grads[i][:], passes)
+            words = gq[i][:].rearrange("p u w -> p (u w)").bitcast(F32).rearrange("p (u w) -> p u w", u=BLOCKS)
+            k_onto_partitions(
+                nc, flip_psum, grad_grouped[i][:], identity[:], lambda g, u: words[:, u, g * P : (g + 1) * P], passes
+            )
 
         def flip_weight(j):
             pair, member = divmod(j, PAIR)
             grouped = weight_grouped[pair][:, :, member * P : (member + 1) * P, :]
-            k_onto_partitions(nc, flip_psum, grouped, identity[:], weights[j][:], both_passes)
+            words = weights[j][:].bitcast(F32)
+            k_onto_partitions(
+                nc,
+                flip_psum,
+                grouped,
+                identity[:],
+                lambda g, u: words[:, g * BLOCKS * P + u : (g + 1) * BLOCKS * P : BLOCKS],
+                both_passes,
+            )
 
         def quantise_grad(i, passes):
             chosen = slice(passes[0], passes[-1] + 1)
@@ -176,15 +178,20 @@ def tile_fa3mlaattention_pb_s_kernel(tc, x, freqs_cis, w_q, grad_out, out):
                 )
 
         keep_warm(3)
-        cosines(0, slice(0, HEADS // 2))
-        cosines(0, slice(HEADS // 2, HEADS))
-        first_sines()
+        all_heads = slice(0, HEADS)
+        products(0, 0, by_cos, slice(0, HEADS // 2))
+        products(0, 0, by_cos, slice(HEADS // 2, HEADS))
+        products(0, 1, by_sin, all_heads)
         for i in range(1, TOKEN_TILES):
-            cosines(i, slice(0, HEADS))
-            sines(i)
+            products(i, 0, by_cos, all_heads)
+            products(i, 1, by_sin, all_heads)
+        move_plain(0)
+        move_plain(1)
+        move_plain(2)
         sums(nc.gpsimd, 0)
         sums(nc.gpsimd, 1)
         flip_weight(0)
+        move_plain(3)
         keep_warm(1)
         flip_weight(1)
         keep_warm(1)
@@ -225,4 +232,4 @@ def tile_fa3mlaattention_pb_s_kernel(tc, x, freqs_cis, w_q, grad_out, out):
             for part in range(parts):
                 columns = slice(part * C // parts, (part + 1) * C // parts)
                 nc.scalar.copy(out=result[:, columns], in_=acc[:, columns])
-                nc.sync.dma_start(out=out_rows[i * P : (i + 1) * P, columns], in_=result[:, columns])
+                nc.sync.dma_start(out=out_rows[i // POSITION_TILES, i % POSITION_TILES, :, columns], in_=result[:, columns])

@@ -88,7 +88,7 @@ def tile_fa3mlaattention_pb_s_kernel(tc, x, freqs_cis, w_q, grad_out, out):
             for turn_number in range(times):
                 nc.tensor.matmul(warm[:, :P], lhsT=identity[:], rhs=identity[:], start=True, stop=True)
 
-        keep_warm(2)
+        keep_warm(1)
         identity_bf16 = keep.tile([P, P], BF16)
         nc.vector.tensor_copy(out=identity_bf16[:], in_=identity[:])
         minus_identity = keep.tile([P, P], BF16)
@@ -100,6 +100,10 @@ def tile_fa3mlaattention_pb_s_kernel(tc, x, freqs_cis, w_q, grad_out, out):
         pairs = freqs[:].rearrange("p a (j c) -> p c a j", c=2)
         for c, s, sign in ((0, 0, identity_bf16), (0, 1, identity_bf16), (1, 1, identity_bf16), (1, 0, minus_identity)):
             nc.tensor.matmul(table_rows[:, c, :, s, :], lhsT=sign[:], rhs=pairs[:, c], start=True, stop=True)
+
+        signed_sines = keep.tile([P, 2 * NF], BF16)
+        nc.vector.tensor_scalar_mul(out=signed_sines[:, 0:NF], in0=pairs[:, 1, 0], scalar1=-1.0)
+        nc.vector.tensor_copy(out=signed_sines[:, NF : 2 * NF], in_=pairs[:, 1, 0])
 
         gq = [keep.tile([P, BLOCKS, PASSES * P * 2], BF16, name="gq%d" % i) for i in range(TOKEN_TILES)]
         by_cos = [turn.tile([P, BLOCKS, HEADS, NF], F32, name="by_cos") for i in range(TOKEN_TILES)]
@@ -125,6 +129,17 @@ def tile_fa3mlaattention_pb_s_kernel(tc, x, freqs_cis, w_q, grad_out, out):
                 in0=chosen,
                 in1=row.unsqueeze(1).to_broadcast(list(chosen.shape)),
             )
+
+        def sines_on_gpsimd(heads):
+            chosen = grads[0][:].rearrange("p (h d) -> p h d", d=HEAD)[:, heads, PLAIN:HEAD]
+            chosen = chosen.rearrange("p h (x u e) -> p u h x e", u=BLOCKS, e=2)
+            row = signed_sines[:].rearrange("p (x u e) -> p u x e", u=BLOCKS, e=2)
+            for u in range(BLOCKS):
+                nc.gpsimd.tensor_mul(
+                    out=by_sin[0][:, u, heads].rearrange("p h (x e) -> p h x e", e=2),
+                    in0=chosen[:, u],
+                    in1=row[:, u].unsqueeze(1).to_broadcast(list(chosen[:, u].shape)),
+                )
 
         def sums(engine, i):
             out_words = gq[i][:].rearrange("p u (h y) -> p u h y", h=HEADS)[:, :, :, NF : 2 * NF]
@@ -177,19 +192,21 @@ def tile_fa3mlaattention_pb_s_kernel(tc, x, freqs_cis, w_q, grad_out, out):
                     in_=weight_grouped[pair][:, g].rearrange("p r u -> p (r u)").bitcast(BF16),
                 )
 
-        keep_warm(3)
+        keep_warm(4)
         all_heads = slice(0, HEADS)
-        products(0, 0, by_cos, slice(0, HEADS // 2))
-        products(0, 0, by_cos, slice(HEADS // 2, HEADS))
-        products(0, 1, by_sin, all_heads)
+        lower_heads, upper_heads = slice(0, HEADS // 2), slice(HEADS // 2, HEADS)
+        products(0, 0, by_cos, lower_heads)
+        products(0, 0, by_cos, upper_heads)
+        sines_on_gpsimd(upper_heads)
+        products(0, 1, by_sin, lower_heads)
         for i in range(1, TOKEN_TILES):
             products(i, 0, by_cos, all_heads)
             products(i, 1, by_sin, all_heads)
         move_plain(0)
         move_plain(1)
         move_plain(2)
-        sums(nc.gpsimd, 0)
-        sums(nc.gpsimd, 1)
+        for i in range(TOKEN_TILES - 1):
+            sums(nc.gpsimd, i)
         flip_weight(0)
         move_plain(3)
         keep_warm(1)
@@ -198,16 +215,14 @@ def tile_fa3mlaattention_pb_s_kernel(tc, x, freqs_cis, w_q, grad_out, out):
         flip_grad(0, both_passes)
         flip_weight(2)
         keep_warm(1)
-        flip_grad(1, both_passes)
         flip_weight(3)
+        flip_grad(1, both_passes)
         keep_warm(1)
-        sums(nc.vector, 2)
+        quantise_weights(0)
         sums(nc.vector, 3)
         flip_grad(2, both_passes)
-        keep_warm(1)
         for g in range(PASSES):
             flip_grad(3, [g])
-        quantise_weights(0)
         quantise_grad(0, both_passes)
         quantise_weights(1)
         quantise_grad(1, both_passes)
@@ -228,7 +243,7 @@ def tile_fa3mlaattention_pb_s_kernel(tc, x, freqs_cis, w_q, grad_out, out):
                     stop=(g == PASSES - 1),
                 )
             result = turn.tile([P, C], F32)
-            parts = 2 if i == TOKEN_TILES - 1 else 1
+            parts = 2 if i in (0, TOKEN_TILES - 1) else 1
             for part in range(parts):
                 columns = slice(part * C // parts, (part + 1) * C // parts)
                 nc.scalar.copy(out=result[:, columns], in_=acc[:, columns])

@@ -205,8 +205,8 @@ def tile_fa3mlaattention_pb_s_kernel(tc, x, freqs_cis, w_q, grad_out, out):
         move_plain(0)
         move_plain(1)
         move_plain(2)
-        for i in range(TOKEN_TILES - 1):
-            sums(nc.gpsimd, i)
+        sums(nc.gpsimd, 0)
+        sums(nc.gpsimd, 1)
         flip_weight(0)
         move_plain(3)
         keep_warm(1)
@@ -218,11 +218,14 @@ def tile_fa3mlaattention_pb_s_kernel(tc, x, freqs_cis, w_q, grad_out, out):
         flip_weight(3)
         flip_grad(1, both_passes)
         keep_warm(1)
+        sums(nc.vector, 2)
         quantise_weights(0)
         sums(nc.vector, 3)
         flip_grad(2, both_passes)
+        keep_warm(1)
         for g in range(PASSES):
             flip_grad(3, [g])
+        keep_warm(1)
         quantise_grad(0, both_passes)
         quantise_weights(1)
         quantise_grad(1, both_passes)

@@ -55,7 +55,7 @@ def tile_fa3mlaattention_pb_s_kernel(tc, x, freqs_cis, w_q, grad_out, out):
         ctx.enter_context(tc.manual_schedule())
 
         freqs = keep.tile([P, POSITION_TILES, 2 * NF], BF16)
-        nc.scalar.dma_start(out=freqs[:], in_=freqs_cis.rearrange("(p a) j c -> p a (j c)", a=POSITION_TILES))
+        nc.sync.dma_start(out=freqs[:], in_=freqs_cis.rearrange("(p a) j c -> p a (j c)", a=POSITION_TILES))
         grads = [keep.tile([P, K], BF16, name="grad%d" % i) for i in range(TOKEN_TILES)]
         weights = [keep.tile([P, K], BF16, name="weight%d" % j) for j in range(C_TILES)]
 
@@ -102,8 +102,8 @@ def tile_fa3mlaattention_pb_s_kernel(tc, x, freqs_cis, w_q, grad_out, out):
             nc.tensor.matmul(table_rows[:, c, :, s, :], lhsT=sign[:], rhs=pairs[:, c], start=True, stop=True)
 
         signed_sines = keep.tile([P, 2 * NF], BF16)
-        nc.vector.tensor_scalar_mul(out=signed_sines[:, 0:NF], in0=pairs[:, 1, 0], scalar1=-1.0)
-        nc.vector.tensor_copy(out=signed_sines[:, NF : 2 * NF], in_=pairs[:, 1, 0])
+        nc.scalar.mul(signed_sines[:, 0:NF], pairs[:, 1, 0], -1.0)
+        nc.scalar.copy(out=signed_sines[:, NF : 2 * NF], in_=pairs[:, 1, 0])
 
         gq = [keep.tile([P, BLOCKS, PASSES * P * 2], BF16, name="gq%d" % i) for i in range(TOKEN_TILES)]
         by_cos = [turn.tile([P, BLOCKS, HEADS, NF], F32, name="by_cos") for i in range(TOKEN_TILES)]
@@ -222,10 +222,9 @@ def tile_fa3mlaattention_pb_s_kernel(tc, x, freqs_cis, w_q, grad_out, out):
         quantise_weights(0)
         sums(nc.vector, 3)
         flip_grad(2, both_passes)
-        keep_warm(1)
+        keep_warm(2)
         for g in range(PASSES):
             flip_grad(3, [g])
-        keep_warm(1)
         quantise_grad(0, both_passes)
         quantise_weights(1)
         quantise_grad(1, both_passes)

from contextlib import ExitStack

import concourse.mybir as mybir
from concourse.masks import make_identity

BF16 = mybir.dt.bfloat16
F32 = mybir.dt.float32
U32 = mybir.dt.uint32
U8 = mybir.dt.uint8
E5M2_X4 = mybir.dt.float8_e5m2_x4
E4M3_X4 = mybir.dt.float8_e4m3fn_x4

P = 128
POSITIONS = 256
TOKENS = 512
HEADS = 16
HEAD = 64
PLAIN = 32
NF = 16
K = HEADS * HEAD
C = 512
PASSES = K // (4 * P)
BLOCKS = 2
TOKEN_TILES = TOKENS // P
POSITION_TILES = POSITIONS // P
C_TILES = C // P
PAIR = 2

FLOPS = 2 * TOKENS * C * K
BYTES = 2 * (TOKENS * K + C * K + POSITIONS * 2 * NF) + 4 * TOKENS * C


def k_onto_partitions(nc, psum, grouped, identity, block, passes):
    flipped = psum.tile([P, PASSES * BLOCKS, P], F32)
    for at, g in enumerate(passes):
        for u in range(BLOCKS):
            nc.tensor.transpose(flipped[:, at * BLOCKS + u, :], block(g, u), identity)
    nc.scalar.copy(
        out=grouped[:, passes[0] : passes[-1] + 1],
        in_=flipped[:, : len(passes) * BLOCKS].rearrange("p (g u) r -> p g r u", u=BLOCKS),
    )


def tile_fa3mlaattention_pb_s_kernel(tc, x, freqs_cis, w_q, grad_out, out):
    nc = tc.nc
    grad_rows = grad_out.rearrange("b (p a) h d -> b a p (h d)", a=POSITION_TILES)
    out_rows = out.rearrange("b (p a) c -> b a p c", a=POSITION_TILES)

    with ExitStack() as ctx:
        keep = ctx.enter_context(tc.tile_pool(name="keep", bufs=1))
        turn = ctx.enter_context(tc.tile_pool(name="turn", bufs=TOKEN_TILES))
        stage = ctx.enter_context(tc.tile_pool(name="stage", bufs=TOKEN_TILES + C_TILES))
        flip_psum = ctx.enter_context(tc.psum_pool(name="flip_psum", bufs=4))
        acc_psum = ctx.enter_context(tc.psum_pool(name="acc_psum", bufs=TOKEN_TILES))
        ctx.enter_context(tc.manual_schedule())

        freqs = keep.tile([P, POSITION_TILES, 2 * NF], BF16)
        nc.sync.dma_start(out=freqs[:], in_=freqs_cis.rearrange("(p a) j c -> p a (j c)", a=POSITION_TILES))
        grads = [keep.tile([P, K], BF16, name="grad%d" % i) for i in range(TOKEN_TILES)]
        weights = [keep.tile([P, K], BF16, name="weight%d" % j) for j in range(C_TILES)]

        def load_grad(i, columns):
            nc.sync.dma_start(out=grads[i][:, columns], in_=grad_rows[i // POSITION_TILES, i % POSITION_TILES, :, columns])

        def load_weight(j):
            nc.sync.dma_start(out=weights[j][:], in_=w_q[j * P : (j + 1) * P, :])

        load_grad(0, slice(0, K // 2))
        load_grad(0, slice(K // 2, K))
        load_grad(1, slice(0, K))
        load_weight(0)
        load_grad(2, slice(0, K))
        load_weight(1)
        load_grad(3, slice(0, K))
        load_weight(2)
        load_weight(3)

        blank = keep.tile([P, 1], F32)
        nc.vector.memset(blank[:], 0.0)
        blank_copy = keep.tile([P, 1], F32)
        nc.scalar.copy(out=blank_copy[:], in_=blank[:])

        identity = keep.tile([P, P], F32)
        make_identity(nc, identity[:])
        warm = acc_psum.tile([P, C], F32, name="acc")

        def keep_warm(times):
            for turn_number in range(times):
                nc.tensor.matmul(warm[:, :P], lhsT=identity[:], rhs=identity[:], start=True, stop=True)

        keep_warm(1)
        identity_bf16 = keep.tile([P, P], BF16)
        nc.vector.tensor_copy(out=identity_bf16[:], in_=identity[:])
        minus_identity = keep.tile([P, P], BF16)
        nc.vector.tensor_scalar_mul(out=minus_identity[:], in0=identity[:], scalar1=-1.0)
        table = acc_psum.tile([P, C], F32, name="acc")
        table_rows = table[:, : 4 * POSITION_TILES * NF].rearrange(
            "p (c a s j) -> p c a s j", c=2, a=POSITION_TILES, s=2
        )
        pairs = freqs[:].rearrange("p a (j c) -> p c a j", c=2)
        for c, s, sign in ((0, 0, identity_bf16), (0, 1, identity_bf16), (1, 1, identity_bf16), (1, 0, minus_identity)):
            nc.tensor.matmul(table_rows[:, c, :, s, :], lhsT=sign[:], rhs=pairs[:, c], start=True, stop=True)

        signed_sines = keep.tile([P, 2 * NF], BF16)
        nc.scalar.mul(signed_sines[:, 0:NF], pairs[:, 1, 0], -1.0)
        nc.scalar.copy(out=signed_sines[:, NF : 2 * NF], in_=pairs[:, 1, 0])

        gq = [keep.tile([P, BLOCKS, PASSES * P * 2], BF16, name="gq%d" % i) for i in range(TOKEN_TILES)]
        by_cos = [turn.tile([P, BLOCKS, HEADS, NF], F32, name="by_cos") for i in range(TOKEN_TILES)]
        by_sin = [turn.tile([P, BLOCKS, HEADS, NF], F32, name="by_sin") for i in range(TOKEN_TILES)]
        grad_codes = [keep.tile([P, PASSES, P], U32, name="grad_codes%d" % i, align_bytes=64) for i in range(TOKEN_TILES)]
        grad_scales = [keep.tile([P, PASSES, P], U8, name="grad_scales%d" % i, align_bytes=64) for i in range(TOKEN_TILES)]
        weight_codes = keep.tile([P, PASSES, C], U32, align_bytes=64)
        weight_scales = keep.tile([P, PASSES, C], U8, align_bytes=64)
        both_passes = list(range(PASSES))
        grad_grouped = [stage.tile([P, PASSES, P, BLOCKS], F32, name="grouped", align_bytes=64) for g in grads]
        weight_grouped = [
            keep.tile([P, PASSES, PAIR * P, BLOCKS], F32, name="weight_grouped%d" % pair, align_bytes=64)
            for pair in range(C_TILES // PAIR)
        ]

        def products(i, c, into, heads):
            rotated = grads[i][:].rearrange("p (h d) -> p h d", d=HEAD)[:, heads, PLAIN:HEAD]
            row = table_rows[:, c, i % POSITION_TILES].rearrange("p s j -> p (s j)")
            row = row.rearrange("p (x u e) -> p x u e", u=BLOCKS, e=2)
            chosen = rotated.rearrange("p h (x u e) -> p h x u e", u=BLOCKS, e=2)
            nc.vector.tensor_mul(
                out=into[i][:, :, heads].rearrange("p u h (x e) -> p h x u e", e=2),
                in0=chosen,
                in1=row.unsqueeze(1).to_broadcast(list(chosen.shape)),
            )

        def sines_on_gpsimd(heads):
            chosen = grads[0][:].rearrange("p (h d) -> p h d", d=HEAD)[:, heads, PLAIN:HEAD]
            chosen = chosen.rearrange("p h (x u e) -> p u h x e", u=BLOCKS, e=2)
            row = signed_sines[:].rearrange("p (x u e) -> p u x e", u=BLOCKS, e=2)
            for u in range(BLOCKS):
                nc.gpsimd.tensor_mul(
                    out=by_sin[0][:, u, heads].rearrange("p h (x e) -> p h x e", e=2),
                    in0=chosen[:, u],
                    in1=row[:, u].unsqueeze(1).to_broadcast(list(chosen[:, u].shape)),
                )

        def sums(engine, i):
            out_words = gq[i][:].rearrange("p u (h y) -> p u h y", h=HEADS)[:, :, :, NF : 2 * NF]
            engine.tensor_add(
                out=out_words.rearrange("p u h (s y) -> p u h s y", s=2),
                in0=by_cos[i][:].rearrange("p u h (s y) -> p u h s y", s=2),
                in1=by_sin[i][:].rearrange("p u h (s y) -> p u h s y", s=2)[:, :, :, ::-1, :],
            )

        def move_plain(i):
            out_words = gq[i][:].rearrange("p u w -> p (u w)").bitcast(F32)
            nc.scalar.copy(
                out=out_words.rearrange("p (u h x) -> p h x u", u=BLOCKS, h=HEADS)[:, :, 0 : NF // 2, :],
                in_=grads[i][:].bitcast(F32).rearrange("p (h x u) -> p h x u", h=HEADS, u=BLOCKS)[:, :, 0 : NF // 2, :],
            )

        def flip_grad(i, passes):
            words = gq[i][:].rearrange("p u w -> p (u w)").bitcast(F32).rearrange("p (u w) -> p u w", u=BLOCKS)
            k_onto_partitions(
                nc, flip_psum, grad_grouped[i][:], identity[:], lambda g, u: words[:, u, g * P : (g + 1) * P], passes
            )

        def flip_weight(j):
            pair, member = divmod(j, PAIR)
            grouped = weight_grouped[pair][:, :, member * P : (member + 1) * P, :]
            words = weights[j][:].bitcast(F32)
            k_onto_partitions(
                nc,
                flip_psum,
                grouped,
                identity[:],
                lambda g, u: words[:, g * BLOCKS * P + u : (g + 1) * BLOCKS * P : BLOCKS],
                both_passes,
            )

        def quantise_grad(i, passes):
            chosen = slice(passes[0], passes[-1] + 1)
            nc.vector.quantize_mx(
                out=grad_codes[i][:, chosen].rearrange("p g r -> p (g r)").bitcast(E5M2_X4),
                scales=grad_scales[i][:, chosen].rearrange("p g r -> p (g r)"),
                in_=grad_grouped[i][:, chosen].rearrange("p g r u -> p (g r u)").bitcast(BF16),
            )

        def quantise_weights(pair):
            columns = slice(pair * PAIR * P, (pair + 1) * PAIR * P)
            for g in range(PASSES):
                nc.vector.quantize_mx(
                    out=weight_codes[:, g, columns].bitcast(E4M3_X4),
                    scales=weight_scales[:, g, columns],
                    in_=weight_grouped[pair][:, g].rearrange("p r u -> p (r u)").bitcast(BF16),
                )

        keep_warm(4)
        all_heads = slice(0, HEADS)
        lower_heads, upper_heads = slice(0, HEADS // 2), slice(HEADS // 2, HEADS)
        products(0, 0, by_cos, lower_heads)
        products(0, 0, by_cos, upper_heads)
        sines_on_gpsimd(upper_heads)
        products(0, 1, by_sin, lower_heads)
        for i in range(1, TOKEN_TILES):
            products(i, 0, by_cos, all_heads)
            products(i, 1, by_sin, all_heads)
        move_plain(0)
        move_plain(1)
        move_plain(2)
        sums(nc.gpsimd, 0)
        sums(nc.gpsimd, 1)
        flip_weight(0)
        move_plain(3)
        keep_warm(1)
        flip_weight(1)
        keep_warm(1)
        flip_grad(0, both_passes)
        flip_weight(2)
        keep_warm(1)
        flip_weight(3)
        flip_grad(1, both_passes)
        keep_warm(1)
        sums(nc.vector, 2)
        quantise_weights(0)
        sums(nc.vector, 3)
        flip_grad(2, both_passes)
        keep_warm(2)
        for g in range(PASSES):
            flip_grad(3, [g])
        quantise_grad(0, both_passes)
        quantise_weights(1)
        quantise_grad(1, both_passes)
        quantise_grad(2, both_passes)
        for g in range(PASSES):
            quantise_grad(3, [g])

        for i in range(TOKEN_TILES):
            acc = acc_psum.tile([P, C], F32, name="acc")
            for g in range(PASSES):
                nc.tensor.matmul_mx(
                    out=acc[:],
                    lhsT=grad_codes[i][:, g, :].bitcast(E5M2_X4),
                    lhsT_scale=grad_scales[i][:, g, :],
                    rhs=weight_codes[:, g, :].bitcast(E4M3_X4),
                    rhs_scale=weight_scales[:, g, :],
                    start=(g == 0),
                    stop=(g == PASSES - 1),
                )
            result = turn.tile([P, C], F32)
            parts = 2 if i in (0, TOKEN_TILES - 1) else 1
            for part in range(parts):
                columns = slice(part * C // parts, (part + 1) * C // parts)
                nc.scalar.copy(out=result[:, columns], in_=acc[:, columns])
                nc.sync.dma_start(out=out_rows[i // POSITION_TILES, i % POSITION_TILES, :, columns], in_=result[:, columns])
